import numpy as np
import ml_dtypes


def mxq(x, axis, fmt="e4m3"):
    dtype, down = {"e4m3": (ml_dtypes.float8_e4m3fn, 7), "e5m2": (ml_dtypes.float8_e5m2, 14)}[fmt]
    v = np.moveaxis(np.asarray(x, np.float32).astype(ml_dtypes.bfloat16).astype(np.float64), axis, -1)
    blocks = v.reshape(v.shape[:-1] + (-1, 32))
    amax = np.abs(blocks).max(-1, keepdims=True)
    byte = np.maximum(np.where(amax > 0, np.frexp(amax)[1] - 1 + 127, 0) - down, 1)
    scale = np.exp2(byte - 127.0)
    codes = (blocks / scale).astype(np.float32).astype(dtype).astype(np.float64)
    return np.moveaxis((codes * scale).reshape(v.shape), -1, axis)


WIDE = False


def mx_kscale(k):
    if not WIDE:
        return np.ones(k)
    levels = np.array([20, -20, 10, -10, 0])
    a = np.random.permutation(np.resize(levels, k // 512 * 4)).reshape(k // 512, 4)
    idx = np.arange(k)
    return np.exp2(a[idx // 512, idx % 128 // 32])


BF16 = ml_dtypes.bfloat16


def bf(x):
    return np.asarray(x, np.float32).astype(BF16)


def f64(x):
    return np.asarray(x).astype(np.float64)


B, S, C, H, D = 4, 512, 1024, 8, 128
E = H * D


def rope_tables():
    inv_freq = 1.0 / (10000.0 ** (np.arange(0, D, 2) / D))
    emb = np.repeat(np.outer(np.arange(S), inv_freq), 2, axis=1)
    return np.cos(emb), np.sin(emb)


def rope(t, cos, sin):
    tr = t[..., 0::2]
    ti = t[..., 1::2]
    t_rot = np.stack([-ti, tr], axis=-1).reshape(t.shape)
    return t * cos + t_rot * sin


def rope_back(dr, cos, sin):
    a = dr * cos
    b = dr * sin
    be = b[..., 0::2]
    bo = b[..., 1::2]
    return a + np.stack([bo, -be], axis=-1).reshape(dr.shape)


def setup_inputs():
    u = np.repeat(mx_kscale(E)[0::2], 2)
    cos, sin = rope_tables()
    cos, sin = bf(cos), bf(sin)
    x = bf(np.random.standard_normal((B, S, C)))
    W0 = bf(np.random.standard_normal((E, C)) / np.sqrt(C))
    bq = bf(np.random.standard_normal(E) * 0.1)
    g = bf(np.random.standard_normal((B, H, S, D)) * np.exp2(np.random.randint(-12, 1, (B, 1, S, 1))) * 16.0 * u.reshape(1, H, 1, D))
    y = f64(x) @ f64(W0).T + f64(bq)
    r = rope(y.reshape(B, S, H, D).transpose(0, 2, 1, 3), f64(cos), f64(sin))
    return {"x": x, "cos": cos, "sin": sin, "Wq": bf(f64(W0) / u[:, None]), "bq": bq,
            "r": np.asarray(r, np.float32), "grad_out": g}


def reference(x, cos, sin, Wq, bq, r, grad_out):
    dr = f64(grad_out) * (f64(r) > 0.0)
    dt = rope_back(dr, f64(cos), f64(sin))
    dy = dt.transpose(0, 2, 1, 3).reshape(B, S, E)
    return mxq(dy, 2, "e5m2") @ mxq(f64(Wq), 0, "e4m3")

@@ -1,0 +1,185 @@
+import concourse.mybir as mybir
+from concourse.masks import make_identity
+
+F32 = mybir.dt.float32
+BF16 = mybir.dt.bfloat16
+U32 = mybir.dt.uint32
+U8 = mybir.dt.uint8
+E4M3_X4 = mybir.dt.float8_e4m3fn_x4
+E5M2_X4 = mybir.dt.float8_e5m2_x4
+ALU = mybir.AluOpType
+
+B, H, S, D, C = 4, 8, 512, 128, 1024
+E = H * D
+P = 128
+TS = S // P
+PACK = 4
+PASSES = E // (P * PACK)
+N_TILE = 512
+N_TILES = C // N_TILE
+HALF_H = H // 2
+J = D // 2
+
+FLOPS = 2 * B * S * E * C
+BYTES = B * H * S * D * (4 + 2) + E * C * 2 + 2 * S * D * 2 + B * S * C * 4
+
+
+def load_inputs(nc, const, loads, cos, sin, Wq, r, grad_out):
+    cos_sb = const.tile([P, TS * D], BF16)
+    sin_sb = const.tile([P, TS * D], BF16)
+    nc.sync.dma_start(out=cos_sb[:], in_=cos.rearrange("(p t) d -> p (t d)", t=TS))
+    nc.sync.dma_start(out=sin_sb[:], in_=sin.rearrange("(p t) d -> p (t d)", t=TS))
+
+    w_raw = const.tile([P, PASSES, PACK, C], BF16)
+    w_view = Wq.rearrange("(g u p e) c -> p g u (e c)", g=PASSES, u=2, e=2)
+
+    r_sb, g_sb = [], []
+    for b in range(B):
+        r_b = loads.tile([P, H, TS * D], F32, name="r_b")
+        g_b = loads.tile([P, H, TS * D], BF16, name="g_b")
+        r_view = r[b].rearrange("h (p t) d -> p h (t d)", t=TS)
+        g_view = grad_out[b].rearrange("h (p t) d -> p h (t d)", t=TS)
+        for heads in (slice(0, HALF_H), slice(HALF_H, H)):
+            nc.sync.dma_start(out=r_b[:, heads, :], in_=r_view[:, heads, :])
+            nc.sync.dma_start(out=g_b[:, heads, :], in_=g_view[:, heads, :])
+        r_sb.append(r_b)
+        g_sb.append(g_b)
+        if b == 0:
+            for g in range(PASSES):
+                nc.sync.dma_start(
+                    out=w_raw[:, g].rearrange("p (u e) c -> p u (e c)", e=2), in_=w_view[:, g]
+                )
+    return cos_sb, sin_sb, w_raw, r_sb, g_sb
+
+
+def make_rope_tables(nc, const, cos_sb, sin_sb):
+    cos_view = cos_sb[:].rearrange("p (t j e) -> p t e j", t=TS, e=2)
+    sin_view = sin_sb[:].rearrange("p (t j e) -> p t e j", t=TS, e=2)
+    tab_own = const.tile([P, TS, 2, J], BF16)
+    tab_pair = const.tile([P, TS, 2, J], BF16)
+    nc.vector.tensor_copy(out=tab_own[:], in_=cos_view)
+    nc.vector.tensor_scalar_mul(out=tab_pair[:, :, 0, :], in0=sin_view[:, :, 0, :], scalar1=-1.0)
+    nc.vector.tensor_copy(out=tab_pair[:, :, 1, :], in_=sin_view[:, :, 1, :])
+    return tab_own, tab_pair
+
+
+def quantise_weights(nc, const, w_raw):
+    w_grouped = const.tile([P, PASSES, C, PACK], BF16, align_bytes=64)
+    w_codes = const.tile([P, PASSES, C], U32, align_bytes=64)
+    w_scales = const.tile([P, PASSES, C], U8, align_bytes=64)
+    for g in range(PASSES):
+        for cols in (slice(0, C // 2), slice(C // 2, C)):
+            nc.scalar.copy(
+                out=w_grouped[:, g, cols, :].rearrange("p (c i) t -> p c t i", i=4),
+                in_=w_raw[:, g, :, cols].rearrange("p t (c i) -> p c t i", i=4),
+            )
+        nc.vector.quantize_mx(
+            out=w_codes[:, g, :].bitcast(E4M3_X4),
+            scales=w_scales[:, g, :],
+            in_=w_grouped[:, g].rearrange("p c t -> p (c t)"),
+        )
+    return w_codes, w_scales
+
+
+def tile_lineartransformerblock_pa_v_kernel(tc, x, cos, sin, Wq, bq, r, grad_out, out):
+    nc = tc.nc
+    with (
+        tc.tile_pool(name="const", bufs=1) as const,
+        tc.tile_pool(name="loads", bufs=B) as loads,
+        tc.tile_pool(name="work", bufs=3) as work,
+        tc.tile_pool(name="quantised", bufs=2 * TS) as quantised,
+        tc.psum_pool(name="turned", bufs=4) as turned,
+        tc.psum_pool(name="sums", bufs=4) as sums,
+    ):
+        cos_sb, sin_sb, w_raw, r_sb, g_sb = load_inputs(nc, const, loads, cos, sin, Wq, r, grad_out)
+        identity = const.tile([P, P], F32)
+        make_identity(nc, identity[:])
+        tab_own, tab_pair = make_rope_tables(nc, const, cos_sb, sin_sb)
+        w_codes, w_scales = None, None
+
+        for b in range(B):
+            dr = work.tile([P, H, TS, D], BF16, bufs=2)
+            for heads in (slice(0, HALF_H), slice(HALF_H, H)):
+                nc.vector.scalar_tensor_tensor(
+                    out=dr[:, heads].rearrange("p h t d -> p (h t d)"),
+                    in0=r_sb[b][:, heads, :].rearrange("p h f -> p (h f)"),
+                    scalar=0.0,
+                    in1=g_sb[b][:, heads, :].rearrange("p h f -> p (h f)"),
+                    op0=ALU.is_gt,
+                    op1=ALU.mult,
+                )
+
+            dy_codes, dy_scales = [], []
+            for ts in range(TS):
+                dr_view = dr[:, :, ts, :].rearrange("p h (j e) -> p e h j", e=2)
+                prod_own = work.tile([P, 2, H, J], F32)
+                prod_pair = work.tile([P, 2, H, J], F32)
+                nc.vector.tensor_tensor(
+                    out=prod_own[:],
+                    in0=dr_view,
+                    in1=tab_own[:, ts].unsqueeze(2).to_broadcast([P, 2, H, J]),
+                    op=ALU.mult,
+                )
+                nc.vector.tensor_tensor(
+                    out=prod_pair[:],
+                    in0=dr_view,
+                    in1=tab_pair[:, ts].unsqueeze(2).to_broadcast([P, 2, H, J]),
+                    op=ALU.mult,
+                )
+
+                grouped = work.tile([P, PASSES, P, PACK], BF16, align_bytes=64)
+                for g in range(PASSES):
+                    dy_t = turned.tile([P, PACK, P], F32)
+                    for u in range(2):
+                        pair_of_heads = slice(2 * (2 * g + u), 2 * (2 * g + u) + 2)
+                        for e in range(2):
+                            nc.tensor.matmul(
+                                out=dy_t[:, 2 * u + e, :],
+                                lhsT=prod_own[:, e, pair_of_heads, :].rearrange("p h j -> p (h j)"),
+                                rhs=identity[:],
+                                is_transpose=True,
+                                start=True,
+                                stop=False,
+                            )
+                            nc.tensor.matmul(
+                                out=dy_t[:, 2 * u + e, :],
+                                lhsT=prod_pair[:, 1 - e, pair_of_heads, :].rearrange("p h j -> p (h j)"),
+                                rhs=identity[:],
+                                is_transpose=True,
+                                start=False,
+                                stop=True,
+                            )
+                    nc.scalar.copy(out=grouped[:, g], in_=dy_t[:].rearrange("p t s -> p s t"))
+
+                codes = quantised.tile([P, PASSES * P], U32, align_bytes=64)
+                scales = quantised.tile([P, PASSES * P], U8, align_bytes=64)
+                nc.vector.quantize_mx(
+                    out=codes[:].bitcast(E5M2_X4),
+                    scales=scales[:],
+                    in_=grouped[:].rearrange("p g s t -> p (g s t)"),
+                )
+                dy_codes.append(codes)
+                dy_scales.append(scales)
+
+            if b == 0:
+                w_codes, w_scales = quantise_weights(nc, const, w_raw)
+
+            out_view = out[b].rearrange("(p t) c -> p t c", t=TS)
+            for ts in range(TS):
+                out_sb = work.tile([P, C], F32, bufs=4)
+                for n in range(N_TILES):
+                    cols = slice(n * N_TILE, (n + 1) * N_TILE)
+                    acc = sums.tile([P, N_TILE], F32)
+                    for g in range(PASSES):
+                        tokens = slice(g * P, (g + 1) * P)
+                        nc.tensor.matmul_mx(
+                            out=acc[:],
+                            lhsT=dy_codes[ts][:, tokens].bitcast(E5M2_X4),
+                            lhsT_scale=dy_scales[ts][:, tokens],
+                            rhs=w_codes[:, g, cols].bitcast(E4M3_X4),
+                            rhs_scale=w_scales[:, g, cols],
+                            start=(g == 0),
+                            stop=(g == PASSES - 1),
+                        )
+                    nc.scalar.copy(out=out_sb[:, cols], in_=acc[:])
+                nc.sync.dma_start(out=out_view[:, ts, :], in_=out_sb[:])

@@ -52,15 +52,27 @@ def load_inputs(nc, const, loads, cos, sin, Wq, r, grad_out):
     return cos_sb, sin_sb, w_raw, r_sb, g_sb
 
 
-def make_rope_tables(nc, const, cos_sb, sin_sb):
+def make_rope_tables(nc, const, tables, cos_sb, sin_sb):
     cos_view = cos_sb[:].rearrange("p (t j e) -> p t e j", t=TS, e=2)
     sin_view = sin_sb[:].rearrange("p (t j e) -> p t e j", t=TS, e=2)
-    tab_own = const.tile([P, TS, 2, J], BF16)
-    tab_pair = const.tile([P, TS, 2, J], BF16)
-    nc.vector.tensor_copy(out=tab_own[:], in_=cos_view)
-    nc.vector.tensor_scalar_mul(out=tab_pair[:, :, 0, :], in0=sin_view[:, :, 0, :], scalar1=-1.0)
-    nc.vector.tensor_copy(out=tab_pair[:, :, 1, :], in_=sin_view[:, :, 1, :])
-    return tab_own, tab_pair
+    own_sb = const.tile([P, TS, 2, J], BF16)
+    pair_sb = const.tile([P, TS, 2, J], BF16)
+    nc.vector.tensor_copy(out=own_sb[:], in_=cos_view)
+    nc.vector.tensor_scalar_mul(out=pair_sb[:, :, 0, :], in0=sin_view[:, :, 0, :], scalar1=-1.0)
+    nc.vector.tensor_copy(out=pair_sb[:, :, 1, :], in_=sin_view[:, :, 1, :])
+
+    identity_bf16 = const.tile([P, P], BF16)
+    make_identity(nc, identity_bf16[:])
+    both = tables.tile([P, 2, TS, 2, J], BF16)
+    for which, table_sb in enumerate((own_sb, pair_sb)):
+        nc.tensor.matmul(
+            out=both[:, which].rearrange("p t e j -> p (t e j)"),
+            lhsT=identity_bf16[:],
+            rhs=table_sb[:].rearrange("p t e j -> p (t e j)"),
+            start=True,
+            stop=True,
+        )
+    return both[:, 0], both[:, 1]
 
 
 def quantise_weights(nc, const, w_raw):
@@ -88,25 +100,33 @@ def tile_lineartransformerblock_pa_v_kernel(tc, x, cos, sin, Wq, bq, r, grad_out
         tc.tile_pool(name="loads", bufs=B) as loads,
         tc.tile_pool(name="work", bufs=3) as work,
         tc.tile_pool(name="quantised", bufs=2 * TS) as quantised,
+        tc.psum_pool(name="tables", bufs=1) as tables,
         tc.psum_pool(name="turned", bufs=4) as turned,
-        tc.psum_pool(name="sums", bufs=4) as sums,
+        tc.psum_pool(name="sums", bufs=3) as sums,
     ):
         cos_sb, sin_sb, w_raw, r_sb, g_sb = load_inputs(nc, const, loads, cos, sin, Wq, r, grad_out)
         identity = const.tile([P, P], F32)
         make_identity(nc, identity[:])
-        tab_own, tab_pair = make_rope_tables(nc, const, cos_sb, sin_sb)
+        tab_own, tab_pair = make_rope_tables(nc, const, tables, cos_sb, sin_sb)
         w_codes, w_scales = None, None
 
         for b in range(B):
             dr = work.tile([P, H, TS, D], BF16, bufs=2)
             for heads in (slice(0, HALF_H), slice(HALF_H, H)):
-                nc.vector.scalar_tensor_tensor(
-                    out=dr[:, heads].rearrange("p h t d -> p (h t d)"),
+                dr_flat = dr[:, heads].rearrange("p h t d -> p (h t d)")
+                nc.gpsimd.tensor_scalar(
+                    out=dr_flat,
                     in0=r_sb[b][:, heads, :].rearrange("p h f -> p (h f)"),
-                    scalar=0.0,
-                    in1=g_sb[b][:, heads, :].rearrange("p h f -> p (h f)"),
+                    scalar1=0.0,
+                    scalar2=1.0,
                     op0=ALU.is_gt,
                     op1=ALU.mult,
+                )
+                nc.vector.tensor_tensor(
+                    out=dr_flat,
+                    in0=dr_flat,
+                    in1=g_sb[b][:, heads, :].rearrange("p h f -> p (h f)"),
+                    op=ALU.mult,
                 )
 
             dy_codes, dy_scales = [], []

@@ -17,8 +17,17 @@ PACK = 4
 PASSES = E // (P * PACK)
 N_TILE = 512
 N_TILES = C // N_TILE
-HALF_H = H // 2
+HEAD_HALVES = (slice(0, H // 2), slice(H // 2, H))
+CHUNK_TILES = 2
+CHUNKS = B * TS // CHUNK_TILES
+assert PASSES == TS // CHUNK_TILES
 J = D // 2
+TOKEN_TILES = B * TS
+LAG = 2
+WEIGHT_QUARTERS = 4
+WEIGHTS_FROM = 2
+WEIGHTS_READY = WEIGHTS_FROM + WEIGHT_QUARTERS + 1
+CATCH_UP = 2
 
 FLOPS = 2 * B * S * E * C
 BYTES = B * H * S * D * (4 + 2) + E * C * 2 + 2 * S * D * 2 + B * S * C * 4
@@ -34,21 +43,22 @@ def load_inputs(nc, const, loads, cos, sin, Wq, r, grad_out):
     w_view = Wq.rearrange("(g u p e) c -> p g u (e c)", g=PASSES, u=2, e=2)
 
     r_sb, g_sb = [], []
-    for b in range(B):
-        r_b = loads.tile([P, H, TS * D], F32, name="r_b")
-        g_b = loads.tile([P, H, TS * D], BF16, name="g_b")
+    for chunk in range(CHUNKS):
+        b, half = divmod(chunk, TS // CHUNK_TILES)
+        if b == 1:
+            nc.sync.dma_start(
+                out=w_raw[:, half].rearrange("p (u e) c -> p u (e c)", e=2), in_=w_view[:, half]
+            )
+        tokens = slice(half * CHUNK_TILES * D, (half + 1) * CHUNK_TILES * D)
+        r_c = loads.tile([P, H, CHUNK_TILES * D], F32, name="r_c")
+        g_c = loads.tile([P, H, CHUNK_TILES * D], BF16, name="g_c")
         r_view = r[b].rearrange("h (p t) d -> p h (t d)", t=TS)
         g_view = grad_out[b].rearrange("h (p t) d -> p h (t d)", t=TS)
-        for heads in (slice(0, HALF_H), slice(HALF_H, H)):
-            nc.sync.dma_start(out=r_b[:, heads, :], in_=r_view[:, heads, :])
-            nc.sync.dma_start(out=g_b[:, heads, :], in_=g_view[:, heads, :])
-        r_sb.append(r_b)
-        g_sb.append(g_b)
-        if b == 0:
-            for g in range(PASSES):
-                nc.sync.dma_start(
-                    out=w_raw[:, g].rearrange("p (u e) c -> p u (e c)", e=2), in_=w_view[:, g]
-                )
+        for heads in HEAD_HALVES:
+            nc.sync.dma_start(out=r_c[:, heads, :], in_=r_view[:, heads, tokens])
+            nc.sync.dma_start(out=g_c[:, heads, :], in_=g_view[:, heads, tokens])
+        r_sb.append(r_c)
+        g_sb.append(g_c)
     return cos_sb, sin_sb, w_raw, r_sb, g_sb
 
 
@@ -72,134 +82,151 @@ def make_rope_tables(nc, const, tables, cos_sb, sin_sb):
             start=True,
             stop=True,
         )
-    return both[:, 0], both[:, 1]
-
-
-def quantise_weights(nc, const, w_raw):
-    w_grouped = const.tile([P, PASSES, C, PACK], BF16, align_bytes=64)
-    w_codes = const.tile([P, PASSES, C], U32, align_bytes=64)
-    w_scales = const.tile([P, PASSES, C], U8, align_bytes=64)
-    for g in range(PASSES):
-        for cols in (slice(0, C // 2), slice(C // 2, C)):
-            nc.scalar.copy(
-                out=w_grouped[:, g, cols, :].rearrange("p (c i) t -> p c t i", i=4),
-                in_=w_raw[:, g, :, cols].rearrange("p t (c i) -> p c t i", i=4),
-            )
-        nc.vector.quantize_mx(
-            out=w_codes[:, g, :].bitcast(E4M3_X4),
-            scales=w_scales[:, g, :],
-            in_=w_grouped[:, g].rearrange("p c t -> p (c t)"),
-        )
-    return w_codes, w_scales
+    return both[:, 0], both[:, 1], pair_sb
 
 
 def tile_lineartransformerblock_pa_v_kernel(tc, x, cos, sin, Wq, bq, r, grad_out, out):
     nc = tc.nc
     with (
         tc.tile_pool(name="const", bufs=1) as const,
-        tc.tile_pool(name="loads", bufs=B) as loads,
-        tc.tile_pool(name="work", bufs=3) as work,
-        tc.tile_pool(name="quantised", bufs=2 * TS) as quantised,
+        tc.tile_pool(name="loads", bufs=CHUNKS) as loads,
+        tc.tile_pool(name="work", bufs=4) as work,
+        tc.tile_pool(name="quantised", bufs=WEIGHTS_READY + 1) as quantised,
         tc.psum_pool(name="tables", bufs=1) as tables,
         tc.psum_pool(name="turned", bufs=4) as turned,
         tc.psum_pool(name="sums", bufs=3) as sums,
+        tc.manual_schedule(),
     ):
         cos_sb, sin_sb, w_raw, r_sb, g_sb = load_inputs(nc, const, loads, cos, sin, Wq, r, grad_out)
         identity = const.tile([P, P], F32)
         make_identity(nc, identity[:])
-        tab_own, tab_pair = make_rope_tables(nc, const, tables, cos_sb, sin_sb)
-        w_codes, w_scales = None, None
+        tab_own, tab_pair, tab_pair_sb = make_rope_tables(nc, const, tables, cos_sb, sin_sb)
+        w_grouped = const.tile([P, PASSES, C, PACK], BF16, align_bytes=64)
+        w_codes = const.tile([P, PASSES, C], U32, align_bytes=64)
+        w_scales = const.tile([P, PASSES, C], U8, align_bytes=64)
 
-        for b in range(B):
-            dr = work.tile([P, H, TS, D], BF16, bufs=2)
-            for heads in (slice(0, HALF_H), slice(HALF_H, H)):
-                dr_flat = dr[:, heads].rearrange("p h t d -> p (h t d)")
-                nc.gpsimd.tensor_scalar(
-                    out=dr_flat,
-                    in0=r_sb[b][:, heads, :].rearrange("p h f -> p (h f)"),
-                    scalar1=0.0,
-                    scalar2=1.0,
-                    op0=ALU.is_gt,
-                    op1=ALU.mult,
-                )
-                nc.vector.tensor_tensor(
-                    out=dr_flat,
-                    in0=dr_flat,
-                    in1=g_sb[b][:, heads, :].rearrange("p h f -> p (h f)"),
-                    op=ALU.mult,
-                )
+        def mask(i):
+            chunk, place = divmod(i, CHUNK_TILES)
+            dr = work.tile([P, H, D], BF16)
+            nc.vector.scalar_tensor_tensor(
+                out=dr[:],
+                in0=r_sb[chunk][:, :, place * D : (place + 1) * D],
+                scalar=0.0,
+                in1=g_sb[chunk][:, :, place * D : (place + 1) * D],
+                op0=ALU.is_gt,
+                op1=ALU.mult,
+            )
+            return dr
 
-            dy_codes, dy_scales = [], []
-            for ts in range(TS):
-                dr_view = dr[:, :, ts, :].rearrange("p h (j e) -> p e h j", e=2)
-                prod_own = work.tile([P, 2, H, J], F32)
-                prod_pair = work.tile([P, 2, H, J], F32)
-                nc.vector.tensor_tensor(
-                    out=prod_own[:],
-                    in0=dr_view,
-                    in1=tab_own[:, ts].unsqueeze(2).to_broadcast([P, 2, H, J]),
-                    op=ALU.mult,
-                )
-                nc.vector.tensor_tensor(
-                    out=prod_pair[:],
-                    in0=dr_view,
-                    in1=tab_pair[:, ts].unsqueeze(2).to_broadcast([P, 2, H, J]),
-                    op=ALU.mult,
-                )
+        def rope_products(dr, ts):
+            dr_view = dr[:].rearrange("p h (j e) -> p e h j", e=2)
+            prod_own = work.tile([P, 2, H, J], F32)
+            prod_pair = work.tile([P, 2, H, J], F32)
+            nc.vector.tensor_tensor(
+                out=prod_own[:],
+                in0=dr_view,
+                in1=tab_own[:, ts].unsqueeze(2).to_broadcast([P, 2, H, J]),
+                op=ALU.mult,
+            )
+            nc.vector.tensor_tensor(
+                out=prod_pair[:, 0],
+                in0=dr_view[:, 0],
+                in1=tab_pair[:, ts, 0].unsqueeze(1).to_broadcast([P, H, J]),
+                op=ALU.mult,
+            )
+            nc.gpsimd.tensor_tensor(
+                out=prod_pair[:, 1],
+                in0=dr_view[:, 1],
+                in1=tab_pair_sb[:, ts, 1].unsqueeze(1).to_broadcast([P, H, J]),
+                op=ALU.mult,
+            )
+            return prod_own, prod_pair
 
-                grouped = work.tile([P, PASSES, P, PACK], BF16, align_bytes=64)
-                for g in range(PASSES):
-                    dy_t = turned.tile([P, PACK, P], F32)
-                    for u in range(2):
-                        pair_of_heads = slice(2 * (2 * g + u), 2 * (2 * g + u) + 2)
-                        for e in range(2):
-                            nc.tensor.matmul(
-                                out=dy_t[:, 2 * u + e, :],
-                                lhsT=prod_own[:, e, pair_of_heads, :].rearrange("p h j -> p (h j)"),
-                                rhs=identity[:],
-                                is_transpose=True,
-                                start=True,
-                                stop=False,
-                            )
-                            nc.tensor.matmul(
-                                out=dy_t[:, 2 * u + e, :],
-                                lhsT=prod_pair[:, 1 - e, pair_of_heads, :].rearrange("p h j -> p (h j)"),
-                                rhs=identity[:],
-                                is_transpose=True,
-                                start=False,
-                                stop=True,
-                            )
-                    nc.scalar.copy(out=grouped[:, g], in_=dy_t[:].rearrange("p t s -> p s t"))
-
-                codes = quantised.tile([P, PASSES * P], U32, align_bytes=64)
-                scales = quantised.tile([P, PASSES * P], U8, align_bytes=64)
-                nc.vector.quantize_mx(
-                    out=codes[:].bitcast(E5M2_X4),
-                    scales=scales[:],
-                    in_=grouped[:].rearrange("p g s t -> p (g s t)"),
-                )
-                dy_codes.append(codes)
-                dy_scales.append(scales)
-
-            if b == 0:
-                w_codes, w_scales = quantise_weights(nc, const, w_raw)
-
-            out_view = out[b].rearrange("(p t) c -> p t c", t=TS)
-            for ts in range(TS):
-                out_sb = work.tile([P, C], F32, bufs=4)
-                for n in range(N_TILES):
-                    cols = slice(n * N_TILE, (n + 1) * N_TILE)
-                    acc = sums.tile([P, N_TILE], F32)
-                    for g in range(PASSES):
-                        tokens = slice(g * P, (g + 1) * P)
-                        nc.tensor.matmul_mx(
-                            out=acc[:],
-                            lhsT=dy_codes[ts][:, tokens].bitcast(E5M2_X4),
-                            lhsT_scale=dy_scales[ts][:, tokens],
-                            rhs=w_codes[:, g, cols].bitcast(E4M3_X4),
-                            rhs_scale=w_scales[:, g, cols],
-                            start=(g == 0),
-                            stop=(g == PASSES - 1),
+        def turn_add_round(prod_own, prod_pair):
+            grouped = work.tile([P, PASSES, P, PACK], BF16, align_bytes=64)
+            for g in range(PASSES):
+                dy_t = turned.tile([P, PACK, P], F32)
+                for u in range(2):
+                    pair_of_heads = slice(2 * (2 * g + u), 2 * (2 * g + u) + 2)
+                    for e in range(2):
+                        nc.tensor.matmul(
+                            out=dy_t[:, 2 * u + e, :],
+                            lhsT=prod_own[:, e, pair_of_heads, :].rearrange("p h j -> p (h j)"),
+                            rhs=identity[:],
+                            is_transpose=True,
+                            start=True,
+                            stop=False,
                         )
-                    nc.scalar.copy(out=out_sb[:, cols], in_=acc[:])
-                nc.sync.dma_start(out=out_view[:, ts, :], in_=out_sb[:])
+                        nc.tensor.matmul(
+                            out=dy_t[:, 2 * u + e, :],
+                            lhsT=prod_pair[:, 1 - e, pair_of_heads, :].rearrange("p h j -> p (h j)"),
+                            rhs=identity[:],
+                            is_transpose=True,
+                            start=False,
+                            stop=True,
+                        )
+                nc.scalar.copy(out=grouped[:, g], in_=dy_t[:].rearrange("p t s -> p s t"))
+            return grouped
+
+        def regroup_weights(quarter):
+            g, half = divmod(quarter, 2)
+            cols = slice(half * (C // 2), (half + 1) * (C // 2))
+            nc.scalar.copy(
+                out=w_grouped[:, g, cols, :].rearrange("p (c i) t -> p c t i", i=4),
+                in_=w_raw[:, g, :, cols].rearrange("p t (c i) -> p c t i", i=4),
+            )
+
+        def quantise_weights():
+            for g in range(PASSES):
+                nc.vector.quantize_mx(
+                    out=w_codes[:, g, :].bitcast(E4M3_X4),
+                    scales=w_scales[:, g, :],
+                    in_=w_grouped[:, g].rearrange("p c t -> p (c t)"),
+                )
+
+        def quantise_dy(grouped):
+            codes = quantised.tile([P, PASSES * P], U32, align_bytes=64)
+            scales = quantised.tile([P, PASSES * P], U8, align_bytes=64)
+            nc.vector.quantize_mx(
+                out=codes[:].bitcast(E5M2_X4),
+                scales=scales[:],
+                in_=grouped[:].rearrange("p g s t -> p (g s t)"),
+            )
+            return codes, scales
+
+        def multiply_and_store(i, codes, scales):
+            b, ts = divmod(i, TS)
+            out_sb = work.tile([P, C], F32)
+            for n in range(N_TILES):
+                cols = slice(n * N_TILE, (n + 1) * N_TILE)
+                acc = sums.tile([P, N_TILE], F32)
+                for g in range(PASSES):
+                    tokens = slice(g * P, (g + 1) * P)
+                    nc.tensor.matmul_mx(
+                        out=acc[:],
+                        lhsT=codes[:, tokens].bitcast(E5M2_X4),
+                        lhsT_scale=scales[:, tokens],
+                        rhs=w_codes[:, g, cols].bitcast(E4M3_X4),
+                        rhs_scale=w_scales[:, g, cols],
+                        start=(g == 0),
+                        stop=(g == PASSES - 1),
+                    )
+                nc.scalar.copy(out=out_sb[:, cols], in_=acc[:])
+            nc.sync.dma_start(out=out[b].rearrange("(p t) c -> p t c", t=TS)[:, ts, :], in_=out_sb[:])
+
+        grouped_of = {}
+        waiting = []
+        for i in range(TOKEN_TILES + LAG):
+            if i < TOKEN_TILES:
+                grouped_of[i] = turn_add_round(*rope_products(mask(i), i % TS))
+            if WEIGHTS_FROM <= i < WEIGHTS_FROM + WEIGHT_QUARTERS:
+                regroup_weights(i - WEIGHTS_FROM)
+            if i >= LAG:
+                waiting.append((i - LAG, quantise_dy(grouped_of[i - LAG])))
+            if i == WEIGHTS_READY:
+                quantise_weights()
+            if i >= WEIGHTS_READY:
+                for tile_index, (codes, scales) in waiting[:CATCH_UP]:
+                    multiply_and_store(tile_index, codes, scales)
+                waiting = waiting[CATCH_UP:]
+        assert not waiting

@@ -95,7 +95,6 @@ def tile_lineartransformerblock_pa_v_kernel(tc, x, cos, sin, Wq, bq, r, grad_out
         tc.psum_pool(name="tables", bufs=1) as tables,
         tc.psum_pool(name="turned", bufs=4) as turned,
         tc.psum_pool(name="sums", bufs=3) as sums,
-        tc.manual_schedule(),
     ):
         cos_sb, sin_sb, w_raw, r_sb, g_sb = load_inputs(nc, const, loads, cos, sin, Wq, r, grad_out)
         identity = const.tile([P, P], F32)

@@ -8,6 +8,7 @@ U8 = mybir.dt.uint8
 E4M3_X4 = mybir.dt.float8_e4m3fn_x4
 E5M2_X4 = mybir.dt.float8_e5m2_x4
 ALU = mybir.AluOpType
+ACT = mybir.ActivationFunctionType
 
 B, H, S, D, C = 4, 8, 512, 128, 1024
 E = H * D
@@ -15,19 +16,29 @@ P = 128
 TS = S // P
 PACK = 4
 PASSES = E // (P * PACK)
+HP = H // PASSES
 N_TILE = 512
 N_TILES = C // N_TILE
-HEAD_HALVES = (slice(0, H // 2), slice(H // 2, H))
-CHUNK_TILES = 2
-CHUNKS = B * TS // CHUNK_TILES
-assert PASSES == TS // CHUNK_TILES
 J = D // 2
-TOKEN_TILES = B * TS
+TU = 2
+HALVES = TS // TU
+UNITS = [
+    (b, g, tp)
+    for b in range(B)
+    for g, tp in (
+        [(g, tp) for g in range(PASSES) for tp in range(HALVES)]
+        if b < B - 1
+        else [(g, tp) for tp in range(HALVES) for g in range(PASSES)]
+    )
+]
 LAG = 2
 WEIGHT_QUARTERS = 4
-WEIGHTS_FROM = 2
-WEIGHTS_READY = WEIGHTS_FROM + WEIGHT_QUARTERS + 1
+WEIGHTS_FROM = 3
+WEIGHTS_READY = WEIGHTS_FROM + WEIGHT_QUARTERS
 CATCH_UP = 2
+SCALAR_MASKS = range(0)
+STEEP = 2.0**100
+STEP_BIAS = 64.0
 
 FLOPS = 2 * B * S * E * C
 BYTES = B * H * S * D * (4 + 2) + E * C * 2 + 2 * S * D * 2 + B * S * C * 4
@@ -36,30 +47,38 @@ BYTES = B * H * S * D * (4 + 2) + E * C * 2 + 2 * S * D * 2 + B * S * C * 4
 def load_inputs(nc, const, loads, cos, sin, Wq, r, grad_out):
     cos_sb = const.tile([P, TS * D], BF16)
     sin_sb = const.tile([P, TS * D], BF16)
-    nc.sync.dma_start(out=cos_sb[:], in_=cos.rearrange("(p t) d -> p (t d)", t=TS))
-    nc.sync.dma_start(out=sin_sb[:], in_=sin.rearrange("(p t) d -> p (t d)", t=TS))
-
     w_raw = const.tile([P, PASSES, PACK, C], BF16)
     w_view = Wq.rearrange("(g u p e) c -> p g u (e c)", g=PASSES, u=2, e=2)
+    sources = {}
 
-    r_sb, g_sb = [], []
-    for chunk in range(CHUNKS):
-        b, half = divmod(chunk, TS // CHUNK_TILES)
-        if b == 1:
-            nc.sync.dma_start(
-                out=w_raw[:, half].rearrange("p (u e) c -> p u (e c)", e=2), in_=w_view[:, half]
-            )
-        tokens = slice(half * CHUNK_TILES * D, (half + 1) * CHUNK_TILES * D)
-        r_c = loads.tile([P, H, CHUNK_TILES * D], F32, name="r_c")
-        g_c = loads.tile([P, H, CHUNK_TILES * D], BF16, name="g_c")
-        r_view = r[b].rearrange("h (p t) d -> p h (t d)", t=TS)
-        g_view = grad_out[b].rearrange("h (p t) d -> p h (t d)", t=TS)
-        for heads in HEAD_HALVES:
-            nc.sync.dma_start(out=r_c[:, heads, :], in_=r_view[:, heads, tokens])
-            nc.sync.dma_start(out=g_c[:, heads, :], in_=g_view[:, heads, tokens])
-        r_sb.append(r_c)
-        g_sb.append(g_c)
-    return cos_sb, sin_sb, w_raw, r_sb, g_sb
+    def load(b, g, halves):
+        heads = slice(g * HP, (g + 1) * HP)
+        tokens = slice(halves[0] * TU * D, (halves[-1] + 1) * TU * D)
+        width = len(halves) * TU * D
+        r_c = loads.tile([P, HP, width], F32, name=f"r_{b}_{g}_{halves[0]}")
+        g_c = loads.tile([P, HP, width], BF16, name=f"g_{b}_{g}_{halves[0]}")
+        nc.sync.dma_start(out=r_c[:], in_=r[b].rearrange("h (p t) d -> p h (t d)", t=TS)[:, heads, tokens])
+        nc.sync.dma_start(out=g_c[:], in_=grad_out[b].rearrange("h (p t) d -> p h (t d)", t=TS)[:, heads, tokens])
+        for k, tp in enumerate(halves):
+            cols = slice(k * TU * D, (k + 1) * TU * D)
+            sources[b, g, tp] = (r_c[:, :, cols], g_c[:, :, cols])
+
+    def load_weights(g):
+        nc.sync.dma_start(out=w_raw[:, g].rearrange("p (u e) c -> p u (e c)", e=2), in_=w_view[:, g])
+
+    load(0, 0, (0,))
+    nc.sync.dma_start(out=cos_sb[:], in_=cos.rearrange("(p t) d -> p (t d)", t=TS))
+    nc.sync.dma_start(out=sin_sb[:], in_=sin.rearrange("(p t) d -> p (t d)", t=TS))
+    load(0, 0, (1,))
+    load(0, 1, (0, 1))
+    load_weights(0)
+    load(1, 0, (0, 1))
+    load_weights(1)
+    load(1, 1, (0, 1))
+    for b in range(2, B):
+        for g in range(PASSES):
+            load(b, g, (0, 1))
+    return cos_sb, sin_sb, w_raw, sources
 
 
 def make_rope_tables(nc, const, tables, cos_sb, sin_sb):
@@ -67,12 +86,11 @@ def make_rope_tables(nc, const, tables, cos_sb, sin_sb):
     sin_view = sin_sb[:].rearrange("p (t j e) -> p t e j", t=TS, e=2)
     own_sb = const.tile([P, TS, 2, J], BF16)
     pair_sb = const.tile([P, TS, 2, J], BF16)
-    nc.vector.tensor_copy(out=own_sb[:], in_=cos_view)
-    nc.vector.tensor_scalar_mul(out=pair_sb[:, :, 0, :], in0=sin_view[:, :, 0, :], scalar1=-1.0)
-    nc.vector.tensor_copy(out=pair_sb[:, :, 1, :], in_=sin_view[:, :, 1, :])
-
     identity_bf16 = const.tile([P, P], BF16)
     make_identity(nc, identity_bf16[:])
+    nc.scalar.copy(out=own_sb[:], in_=cos_view)
+    nc.scalar.copy(out=pair_sb[:, :, 1, :], in_=sin_view[:, :, 1, :])
+    nc.scalar.activation(out=pair_sb[:, :, 0, :], in_=sin_view[:, :, 0, :], func=ACT.Copy, scale=-1.0)
     both = tables.tile([P, 2, TS, 2, J], BF16)
     for which, table_sb in enumerate((own_sb, pair_sb)):
         nc.tensor.matmul(
@@ -89,68 +107,72 @@ def tile_lineartransformerblock_pa_v_kernel(tc, x, cos, sin, Wq, bq, r, grad_out
     nc = tc.nc
     with (
         tc.tile_pool(name="const", bufs=1) as const,
-        tc.tile_pool(name="loads", bufs=CHUNKS) as loads,
+        tc.tile_pool(name="loads", bufs=1) as loads,
         tc.tile_pool(name="work", bufs=4) as work,
-        tc.tile_pool(name="quantised", bufs=WEIGHTS_READY + 1) as quantised,
+        tc.tile_pool(name="quantised", bufs=14) as quantised,
         tc.psum_pool(name="tables", bufs=1) as tables,
         tc.psum_pool(name="turned", bufs=4) as turned,
         tc.psum_pool(name="sums", bufs=3) as sums,
     ):
-        cos_sb, sin_sb, w_raw, r_sb, g_sb = load_inputs(nc, const, loads, cos, sin, Wq, r, grad_out)
+        cos_sb, sin_sb, w_raw, sources = load_inputs(nc, const, loads, cos, sin, Wq, r, grad_out)
+        tab_own, tab_pair, tab_pair_sb = make_rope_tables(nc, const, tables, cos_sb, sin_sb)
         identity = const.tile([P, P], F32)
         make_identity(nc, identity[:])
-        tab_own, tab_pair, tab_pair_sb = make_rope_tables(nc, const, tables, cos_sb, sin_sb)
         w_grouped = const.tile([P, PASSES, C, PACK], BF16, align_bytes=64)
         w_codes = const.tile([P, PASSES, C], U32, align_bytes=64)
         w_scales = const.tile([P, PASSES, C], U8, align_bytes=64)
 
-        def mask(i):
-            chunk, place = divmod(i, CHUNK_TILES)
-            dr = work.tile([P, H, D], BF16)
-            nc.vector.scalar_tensor_tensor(
-                out=dr[:],
-                in0=r_sb[chunk][:, :, place * D : (place + 1) * D],
-                scalar=0.0,
-                in1=g_sb[chunk][:, :, place * D : (place + 1) * D],
-                op0=ALU.is_gt,
-                op1=ALU.mult,
-            )
+        def mask(k):
+            r_u, g_u = (view.rearrange("p h (t d) -> p h t d", t=TU) for view in sources[UNITS[k]])
+            dr = work.tile([P, TU, HP, D], BF16)
+            dr_out = dr[:].rearrange("p t h d -> p h t d")
+            if k in SCALAR_MASKS:
+                positive = work.tile([P, TU, HP, D], BF16)
+                pos_view = positive[:].rearrange("p t h d -> p h t d")
+                nc.scalar.activation(out=pos_view, in_=r_u, func=ACT.Sigmoid, scale=STEEP, bias=-STEP_BIAS)
+                nc.vector.tensor_tensor(out=dr_out, in0=pos_view, in1=g_u, op=ALU.mult)
+            else:
+                for t in range(TU):
+                    nc.vector.scalar_tensor_tensor(
+                        out=dr[:, t], in0=r_u[:, :, t], scalar=0.0, in1=g_u[:, :, t], op0=ALU.is_gt, op1=ALU.mult
+                    )
             return dr
 
-        def rope_products(dr, ts):
-            dr_view = dr[:].rearrange("p h (j e) -> p e h j", e=2)
-            prod_own = work.tile([P, 2, H, J], F32)
-            prod_pair = work.tile([P, 2, H, J], F32)
+        def rope_products(k, dr):
+            tokens = slice(UNITS[k][2] * TU, (UNITS[k][2] + 1) * TU)
+            dr_view = dr[:].rearrange("p t h (j e) -> p t e h j", e=2)
+            prod_own = work.tile([P, TU, 2, HP, J], F32)
+            prod_pair = work.tile([P, 2, TU, HP, J], F32)
             nc.vector.tensor_tensor(
                 out=prod_own[:],
                 in0=dr_view,
-                in1=tab_own[:, ts].unsqueeze(2).to_broadcast([P, 2, H, J]),
+                in1=tab_own[:, tokens].unsqueeze(3).to_broadcast([P, TU, 2, HP, J]),
                 op=ALU.mult,
             )
             nc.vector.tensor_tensor(
                 out=prod_pair[:, 0],
-                in0=dr_view[:, 0],
-                in1=tab_pair[:, ts, 0].unsqueeze(1).to_broadcast([P, H, J]),
+                in0=dr_view[:, :, 0],
+                in1=tab_pair[:, tokens, 0].unsqueeze(2).to_broadcast([P, TU, HP, J]),
                 op=ALU.mult,
             )
             nc.gpsimd.tensor_tensor(
                 out=prod_pair[:, 1],
-                in0=dr_view[:, 1],
-                in1=tab_pair_sb[:, ts, 1].unsqueeze(1).to_broadcast([P, H, J]),
+                in0=dr_view[:, :, 1],
+                in1=tab_pair_sb[:, tokens, 1].unsqueeze(2).to_broadcast([P, TU, HP, J]),
                 op=ALU.mult,
             )
             return prod_own, prod_pair
 
         def turn_add_round(prod_own, prod_pair):
-            grouped = work.tile([P, PASSES, P, PACK], BF16, align_bytes=64)
-            for g in range(PASSES):
+            grouped = work.tile([P, TU, P, PACK], BF16, align_bytes=64)
+            for t in range(TU):
                 dy_t = turned.tile([P, PACK, P], F32)
                 for u in range(2):
-                    pair_of_heads = slice(2 * (2 * g + u), 2 * (2 * g + u) + 2)
+                    heads = slice(2 * u, 2 * u + 2)
                     for e in range(2):
                         nc.tensor.matmul(
                             out=dy_t[:, 2 * u + e, :],
-                            lhsT=prod_own[:, e, pair_of_heads, :].rearrange("p h j -> p (h j)"),
+                            lhsT=prod_own[:, t, e, heads, :].rearrange("p h j -> p (h j)"),
                             rhs=identity[:],
                             is_transpose=True,
                             start=True,
@@ -158,13 +180,13 @@ def tile_lineartransformerblock_pa_v_kernel(tc, x, cos, sin, Wq, bq, r, grad_out
                         )
                         nc.tensor.matmul(
                             out=dy_t[:, 2 * u + e, :],
-                            lhsT=prod_pair[:, 1 - e, pair_of_heads, :].rearrange("p h j -> p (h j)"),
+                            lhsT=prod_pair[:, 1 - e, t, heads, :].rearrange("p h j -> p (h j)"),
                             rhs=identity[:],
                             is_transpose=True,
                             start=False,
                             stop=True,
                         )
-                nc.scalar.copy(out=grouped[:, g], in_=dy_t[:].rearrange("p t s -> p s t"))
+                nc.scalar.copy(out=grouped[:, t], in_=dy_t[:].rearrange("p w s -> p s w"))
             return grouped
 
         def regroup_weights(quarter):
@@ -175,32 +197,31 @@ def tile_lineartransformerblock_pa_v_kernel(tc, x, cos, sin, Wq, bq, r, grad_out
                 in_=w_raw[:, g, :, cols].rearrange("p t (c i) -> p c t i", i=4),
             )
 
-        def quantise_weights():
-            for g in range(PASSES):
-                nc.vector.quantize_mx(
-                    out=w_codes[:, g, :].bitcast(E4M3_X4),
-                    scales=w_scales[:, g, :],
-                    in_=w_grouped[:, g].rearrange("p c t -> p (c t)"),
-                )
+        def quantise_weights(g):
+            nc.vector.quantize_mx(
+                out=w_codes[:, g, :].bitcast(E4M3_X4),
+                scales=w_scales[:, g, :],
+                in_=w_grouped[:, g].rearrange("p c t -> p (c t)"),
+            )
 
         def quantise_dy(grouped):
-            codes = quantised.tile([P, PASSES * P], U32, align_bytes=64)
-            scales = quantised.tile([P, PASSES * P], U8, align_bytes=64)
+            codes = quantised.tile([P, TU * P], U32, align_bytes=64)
+            scales = quantised.tile([P, TU * P], U8, align_bytes=64)
             nc.vector.quantize_mx(
                 out=codes[:].bitcast(E5M2_X4),
                 scales=scales[:],
-                in_=grouped[:].rearrange("p g s t -> p (g s t)"),
+                in_=grouped[:].rearrange("p t s w -> p (t s w)"),
             )
             return codes, scales
 
-        def multiply_and_store(i, codes, scales):
-            b, ts = divmod(i, TS)
+        def multiply_and_store(b, ts, operands):
             out_sb = work.tile([P, C], F32)
+            tokens = slice(ts % TU * P, (ts % TU + 1) * P)
             for n in range(N_TILES):
                 cols = slice(n * N_TILE, (n + 1) * N_TILE)
                 acc = sums.tile([P, N_TILE], F32)
                 for g in range(PASSES):
-                    tokens = slice(g * P, (g + 1) * P)
+                    codes, scales = operands[g]
                     nc.tensor.matmul_mx(
                         out=acc[:],
                         lhsT=codes[:, tokens].bitcast(E5M2_X4),
@@ -214,18 +235,25 @@ def tile_lineartransformerblock_pa_v_kernel(tc, x, cos, sin, Wq, bq, r, grad_out
             nc.sync.dma_start(out=out[b].rearrange("(p t) c -> p t c", t=TS)[:, ts, :], in_=out_sb[:])
 
         grouped_of = {}
+        quantised_of = {}
         waiting = []
-        for i in range(TOKEN_TILES + LAG):
-            if i < TOKEN_TILES:
-                grouped_of[i] = turn_add_round(*rope_products(mask(i), i % TS))
-            if WEIGHTS_FROM <= i < WEIGHTS_FROM + WEIGHT_QUARTERS:
-                regroup_weights(i - WEIGHTS_FROM)
-            if i >= LAG:
-                waiting.append((i - LAG, quantise_dy(grouped_of[i - LAG])))
-            if i == WEIGHTS_READY:
-                quantise_weights()
-            if i >= WEIGHTS_READY:
-                for tile_index, (codes, scales) in waiting[:CATCH_UP]:
-                    multiply_and_store(tile_index, codes, scales)
+        for step in range(len(UNITS) + LAG):
+            if step < len(UNITS):
+                grouped_of[step] = turn_add_round(*rope_products(step, mask(step)))
+            if WEIGHTS_FROM <= step < WEIGHTS_READY:
+                regroup_weights(step - WEIGHTS_FROM)
+            if step >= LAG:
+                b, g, tp = UNITS[step - LAG]
+                quantised_of[b, g, tp] = quantise_dy(grouped_of[step - LAG])
+                if all((b, other, tp) in quantised_of for other in range(PASSES)):
+                    for ts in range(tp * TU, (tp + 1) * TU):
+                        waiting.append((b, ts, [quantised_of[b, other, tp] for other in range(PASSES)]))
+            if step == WEIGHTS_READY:
+                for g in range(PASSES):
+                    quantise_weights(g)
+            if step >= WEIGHTS_READY:
+                for job in waiting[:CATCH_UP]:
+                    multiply_and_store(*job)
                 waiting = waiting[CATCH_UP:]
-        assert not waiting
+        for job in waiting:
+            multiply_and_store(*job)

@@ -19,26 +19,25 @@ PASSES = E // (P * PACK)
 HP = H // PASSES
 N_TILE = 512
 N_TILES = C // N_TILE
-J = D // 2
-TU = 2
-HALVES = TS // TU
-UNITS = [
-    (b, g, tp)
-    for b in range(B)
-    for g, tp in (
-        [(g, tp) for g in range(PASSES) for tp in range(HALVES)]
-        if b < B - 1
-        else [(g, tp) for tp in range(HALVES) for g in range(PASSES)]
-    )
-]
+
+UNITS = (
+    [(0, (g,), (0, 1)) for g in range(PASSES)]
+    + [(b, (0, 1), (ts,)) for b in range(B) for ts in range(TS) if (b, ts) not in ((0, 0), (0, 1), (3, 3))]
+    + [(3, (g,), (3,)) for g in range(PASSES)]
+)
+LOADS = (
+    [(0, (0,), (0, 1)), (0, (1,), (0, 1)), (0, (0, 1), (2, 3)), 0, 1]
+    + [(1, (0, 1), (0, 1)), (1, (0, 1), (2, 3))]
+    + [(b, (0, 1), (0, 1, 2, 3)) for b in (2, 3)]
+)
 LAG = 2
-WEIGHT_QUARTERS = 4
-WEIGHTS_FROM = 3
-WEIGHTS_READY = WEIGHTS_FROM + WEIGHT_QUARTERS
-CATCH_UP = 2
-SCALAR_MASKS = range(0)
+STEPS = len(UNITS) + LAG
+SCALAR_MASKS = (1, 2, 6, 9, 12)
+MASK_LEAD = 1
 STEEP = 2.0**100
 STEP_BIAS = 64.0
+REGROUP_STEP = (1, 1, 2, 2)
+QUANTISE_STEP = (4, 5)
 
 FLOPS = 2 * B * S * E * C
 BYTES = B * H * S * D * (4 + 2) + E * C * 2 + 2 * S * D * 2 + B * S * C * 4
@@ -47,59 +46,37 @@ BYTES = B * H * S * D * (4 + 2) + E * C * 2 + 2 * S * D * 2 + B * S * C * 4
 def load_inputs(nc, const, loads, cos, sin, Wq, r, grad_out):
     cos_sb = const.tile([P, TS * D], BF16)
     sin_sb = const.tile([P, TS * D], BF16)
-    w_raw = const.tile([P, PASSES, PACK, C], BF16)
-    w_view = Wq.rearrange("(g u p e) c -> p g u (e c)", g=PASSES, u=2, e=2)
-    sources = {}
-
-    def load(b, g, halves):
-        heads = slice(g * HP, (g + 1) * HP)
-        tokens = slice(halves[0] * TU * D, (halves[-1] + 1) * TU * D)
-        width = len(halves) * TU * D
-        r_c = loads.tile([P, HP, width], F32, name=f"r_{b}_{g}_{halves[0]}")
-        g_c = loads.tile([P, HP, width], BF16, name=f"g_{b}_{g}_{halves[0]}")
-        nc.sync.dma_start(out=r_c[:], in_=r[b].rearrange("h (p t) d -> p h (t d)", t=TS)[:, heads, tokens])
-        nc.sync.dma_start(out=g_c[:], in_=grad_out[b].rearrange("h (p t) d -> p h (t d)", t=TS)[:, heads, tokens])
-        for k, tp in enumerate(halves):
-            cols = slice(k * TU * D, (k + 1) * TU * D)
-            sources[b, g, tp] = (r_c[:, :, cols], g_c[:, :, cols])
-
-    def load_weights(g):
-        nc.sync.dma_start(out=w_raw[:, g].rearrange("p (u e) c -> p u (e c)", e=2), in_=w_view[:, g])
-
-    load(0, 0, (0,))
     nc.sync.dma_start(out=cos_sb[:], in_=cos.rearrange("(p t) d -> p (t d)", t=TS))
     nc.sync.dma_start(out=sin_sb[:], in_=sin.rearrange("(p t) d -> p (t d)", t=TS))
-    load(0, 0, (1,))
-    load(0, 1, (0, 1))
-    load_weights(0)
-    load(1, 0, (0, 1))
-    load_weights(1)
-    load(1, 1, (0, 1))
-    for b in range(2, B):
-        for g in range(PASSES):
-            load(b, g, (0, 1))
-    return cos_sb, sin_sb, w_raw, sources
+    w_raw = const.tile([P, PASSES, PACK, C], BF16)
+    w_view = Wq.rearrange("(g h p) c -> p g h c", g=PASSES, h=PACK)
+    r_sb = [loads.tile([P, H, TS * D], F32, name=f"r_{b}") for b in range(B)]
+    g_sb = [loads.tile([P, H, TS * D], BF16, name=f"g_{b}") for b in range(B)]
+    for item in LOADS:
+        if isinstance(item, int):
+            nc.sync.dma_start(out=w_raw[:, item], in_=w_view[:, item])
+            continue
+        b, passes, tokens = item
+        cols = slice(tokens[0] * D, (tokens[-1] + 1) * D)
+        for g in passes:
+            heads = slice(g * HP, (g + 1) * HP)
+            for tile, src in ((r_sb[b], r), (g_sb[b], grad_out)):
+                view = src[b].rearrange("h (p t) d -> p h (t d)", t=TS)
+                nc.sync.dma_start(out=tile[:, heads, cols], in_=view[:, heads, cols])
+    return cos_sb, sin_sb, w_raw, r_sb, g_sb
 
 
 def make_rope_tables(nc, const, tables, cos_sb, sin_sb):
-    cos_view = cos_sb[:].rearrange("p (t j e) -> p t e j", t=TS, e=2)
-    sin_view = sin_sb[:].rearrange("p (t j e) -> p t e j", t=TS, e=2)
-    own_sb = const.tile([P, TS, 2, J], BF16)
-    pair_sb = const.tile([P, TS, 2, J], BF16)
+    pair_sb = const.tile([P, TS * D], BF16)
+    pair_view = pair_sb[:].rearrange("p (n e) -> p n e", e=2)
+    sin_view = sin_sb[:].rearrange("p (n e) -> p n e", e=2)
     identity_bf16 = const.tile([P, P], BF16)
     make_identity(nc, identity_bf16[:])
-    nc.scalar.copy(out=own_sb[:], in_=cos_view)
-    nc.scalar.copy(out=pair_sb[:, :, 1, :], in_=sin_view[:, :, 1, :])
-    nc.scalar.activation(out=pair_sb[:, :, 0, :], in_=sin_view[:, :, 0, :], func=ACT.Copy, scale=-1.0)
-    both = tables.tile([P, 2, TS, 2, J], BF16)
-    for which, table_sb in enumerate((own_sb, pair_sb)):
-        nc.tensor.matmul(
-            out=both[:, which].rearrange("p t e j -> p (t e j)"),
-            lhsT=identity_bf16[:],
-            rhs=table_sb[:].rearrange("p t e j -> p (t e j)"),
-            start=True,
-            stop=True,
-        )
+    nc.scalar.copy(out=pair_view[:, :, 0], in_=sin_view[:, :, 1])
+    nc.scalar.activation(out=pair_view[:, :, 1], in_=sin_view[:, :, 0], func=ACT.Copy, scale=-1.0)
+    both = tables.tile([P, 2, TS * D], BF16)
+    for which, table_sb in enumerate((cos_sb, pair_sb)):
+        nc.tensor.matmul(out=both[:, which], lhsT=identity_bf16[:], rhs=table_sb[:], start=True, stop=True)
     return both[:, 0], both[:, 1], pair_sb
 
 
@@ -109,12 +86,13 @@ def tile_lineartransformerblock_pa_v_kernel(tc, x, cos, sin, Wq, bq, r, grad_out
         tc.tile_pool(name="const", bufs=1) as const,
         tc.tile_pool(name="loads", bufs=1) as loads,
         tc.tile_pool(name="work", bufs=4) as work,
-        tc.tile_pool(name="quantised", bufs=14) as quantised,
+        tc.tile_pool(name="products", bufs=4) as products,
+        tc.tile_pool(name="quantised", bufs=10) as quantised,
         tc.psum_pool(name="tables", bufs=1) as tables,
         tc.psum_pool(name="turned", bufs=4) as turned,
         tc.psum_pool(name="sums", bufs=3) as sums,
     ):
-        cos_sb, sin_sb, w_raw, sources = load_inputs(nc, const, loads, cos, sin, Wq, r, grad_out)
+        cos_sb, sin_sb, w_raw, r_sb, g_sb = load_inputs(nc, const, loads, cos, sin, Wq, r, grad_out)
         tab_own, tab_pair, tab_pair_sb = make_rope_tables(nc, const, tables, cos_sb, sin_sb)
         identity = const.tile([P, P], F32)
         make_identity(nc, identity[:])
@@ -122,71 +100,83 @@ def tile_lineartransformerblock_pa_v_kernel(tc, x, cos, sin, Wq, bq, r, grad_out
         w_codes = const.tile([P, PASSES, C], U32, align_bytes=64)
         w_scales = const.tile([P, PASSES, C], U8, align_bytes=64)
 
-        def mask(k):
-            r_u, g_u = (view.rearrange("p h (t d) -> p h t d", t=TU) for view in sources[UNITS[k]])
-            dr = work.tile([P, TU, HP, D], BF16)
-            dr_out = dr[:].rearrange("p t h d -> p h t d")
-            if k in SCALAR_MASKS:
-                positive = work.tile([P, TU, HP, D], BF16)
-                pos_view = positive[:].rearrange("p t h d -> p h t d")
-                nc.scalar.activation(out=pos_view, in_=r_u, func=ACT.Sigmoid, scale=STEEP, bias=-STEP_BIAS)
-                nc.vector.tensor_tensor(out=dr_out, in0=pos_view, in1=g_u, op=ALU.mult)
-            else:
-                for t in range(TU):
-                    nc.vector.scalar_tensor_tensor(
-                        out=dr[:, t], in0=r_u[:, :, t], scalar=0.0, in1=g_u[:, :, t], op0=ALU.is_gt, op1=ALU.mult
-                    )
+        def parts(unit):
+            b, passes, tokens = unit
+            heads = slice(passes[0] * HP, (passes[-1] + 1) * HP)
+            cols = slice(tokens[0] * D, (tokens[-1] + 1) * D)
+            return b, heads, cols, len(passes) * HP, len(tokens)
+
+        positives = {}
+
+        def scalar_mask(unit):
+            b, heads, cols, nh, nt = parts(unit)
+            positives[unit] = work.tile([P, nh, nt * D], BF16, name="positive")
+            nc.scalar.activation(
+                out=positives[unit][:], in_=r_sb[b][:, heads, cols], func=ACT.Sigmoid, scale=STEEP, bias=-STEP_BIAS
+            )
+
+        def mask(unit):
+            b, heads, cols, nh, nt = parts(unit)
+            dr = work.tile([P, nh, nt * D], BF16)
+            if unit in positives:
+                nc.vector.tensor_tensor(
+                    out=dr[:], in0=positives[unit][:], in1=g_sb[b][:, heads, cols], op=ALU.mult
+                )
+                return dr
+            nc.vector.scalar_tensor_tensor(
+                out=dr[:],
+                in0=r_sb[b][:, heads, cols],
+                scalar=0.0,
+                in1=g_sb[b][:, heads, cols],
+                op0=ALU.is_gt,
+                op1=ALU.mult,
+            )
             return dr
 
-        def rope_products(k, dr):
-            tokens = slice(UNITS[k][2] * TU, (UNITS[k][2] + 1) * TU)
-            dr_view = dr[:].rearrange("p t h (j e) -> p t e h j", e=2)
-            prod_own = work.tile([P, TU, 2, HP, J], F32)
-            prod_pair = work.tile([P, 2, TU, HP, J], F32)
+        def rope_products(unit, dr):
+            b, heads, cols, nh, nt = parts(unit)
+            own = products.tile([P, nh, nt * D], F32)
+            pair = products.tile([P, nh, nt * D], F32)
             nc.vector.tensor_tensor(
-                out=prod_own[:],
-                in0=dr_view,
-                in1=tab_own[:, tokens].unsqueeze(3).to_broadcast([P, TU, 2, HP, J]),
+                out=own[:],
+                in0=dr[:],
+                in1=tab_own[:, cols].unsqueeze(1).to_broadcast([P, nh, nt * D]),
                 op=ALU.mult,
             )
-            nc.vector.tensor_tensor(
-                out=prod_pair[:, 0],
-                in0=dr_view[:, :, 0],
-                in1=tab_pair[:, tokens, 0].unsqueeze(2).to_broadcast([P, TU, HP, J]),
-                op=ALU.mult,
-            )
-            nc.gpsimd.tensor_tensor(
-                out=prod_pair[:, 1],
-                in0=dr_view[:, :, 1],
-                in1=tab_pair_sb[:, tokens, 1].unsqueeze(2).to_broadcast([P, TU, HP, J]),
-                op=ALU.mult,
-            )
-            return prod_own, prod_pair
+            swapped = dr[:].rearrange("p h (n e) -> p h n e", e=2)[:, :, :, ::-1]
+            split = nh - nh * 1 // 2
+            for engine, table, hs in (
+                (nc.gpsimd, tab_pair_sb[:], slice(split, nh)),
+                (nc.vector, tab_pair, slice(0, split)),
+            ):
+                engine.tensor_tensor(
+                    out=pair[:, hs].rearrange("p h (n e) -> p h n e", e=2),
+                    in0=swapped[:, hs],
+                    in1=table[:, cols]
+                    .rearrange("p (n e) -> p n e", e=2)
+                    .unsqueeze(1)
+                    .to_broadcast([P, hs.stop - hs.start, nt * D // 2, 2]),
+                    op=ALU.mult,
+                )
+            return own, pair
 
-        def turn_add_round(prod_own, prod_pair):
-            grouped = work.tile([P, TU, P, PACK], BF16, align_bytes=64)
-            for t in range(TU):
-                dy_t = turned.tile([P, PACK, P], F32)
-                for u in range(2):
-                    heads = slice(2 * u, 2 * u + 2)
-                    for e in range(2):
-                        nc.tensor.matmul(
-                            out=dy_t[:, 2 * u + e, :],
-                            lhsT=prod_own[:, t, e, heads, :].rearrange("p h j -> p (h j)"),
-                            rhs=identity[:],
-                            is_transpose=True,
-                            start=True,
-                            stop=False,
-                        )
-                        nc.tensor.matmul(
-                            out=dy_t[:, 2 * u + e, :],
-                            lhsT=prod_pair[:, 1 - e, t, heads, :].rearrange("p h j -> p (h j)"),
-                            rhs=identity[:],
-                            is_transpose=True,
-                            start=False,
-                            stop=True,
-                        )
-                nc.scalar.copy(out=grouped[:, t], in_=dy_t[:].rearrange("p w s -> p s w"))
+        def turn_add_round(unit, own, pair):
+            b, passes, tokens = unit
+            grouped = work.tile([P, len(passes) * len(tokens), P, PACK], BF16, align_bytes=64)
+            for i, g in enumerate(passes):
+                for t in range(len(tokens)):
+                    dy_t = turned.tile([P, PACK, P], F32)
+                    for h in range(HP):
+                        for product, start in ((own, True), (pair, False)):
+                            nc.tensor.matmul(
+                                out=dy_t[:, h, :],
+                                lhsT=product[:, i * HP + h, t * D : (t + 1) * D],
+                                rhs=identity[:],
+                                is_transpose=True,
+                                start=start,
+                                stop=not start,
+                            )
+                    nc.scalar.copy(out=grouped[:, i * len(tokens) + t], in_=dy_t[:].rearrange("p w s -> p s w"))
             return grouped
 
         def regroup_weights(quarter):
@@ -204,56 +194,69 @@ def tile_lineartransformerblock_pa_v_kernel(tc, x, cos, sin, Wq, bq, r, grad_out
                 in_=w_grouped[:, g].rearrange("p c t -> p (c t)"),
             )
 
-        def quantise_dy(grouped):
-            codes = quantised.tile([P, TU * P], U32, align_bytes=64)
-            scales = quantised.tile([P, TU * P], U8, align_bytes=64)
+        def multiply_bank(b, ts, n, operands, copy):
+            cols = slice(n * N_TILE, (n + 1) * N_TILE)
+            if n == 0:
+                out_tiles[b, ts] = work.tile([P, C], F32, name="out_sb")
+            acc = sums.tile([P, N_TILE], F32)
+            for g in range(PASSES):
+                codes, scales, words = operands[g]
+                nc.tensor.matmul_mx(
+                    out=acc[:],
+                    lhsT=codes[:, words].bitcast(E5M2_X4),
+                    lhsT_scale=scales[:, words],
+                    rhs=w_codes[:, g, cols].bitcast(E4M3_X4),
+                    rhs_scale=w_scales[:, g, cols],
+                    start=(g == 0),
+                    stop=(g == PASSES - 1),
+                )
+            copy(out=out_tiles[b, ts][:, cols], in_=acc[:])
+            if n == N_TILES - 1:
+                nc.sync.dma_start(
+                    out=out[b].rearrange("(p t) c -> p t c", t=TS)[:, ts, :], in_=out_tiles[b, ts][:]
+                )
+
+        out_tiles = {}
+        quantised_of = {}
+        waiting = []
+
+        def quantise_unit(unit, grouped):
+            b, passes, tokens = unit
+            n = grouped.shape[1]
+            codes = quantised.tile([P, n * P], U32, align_bytes=64)
+            scales = quantised.tile([P, n * P], U8, align_bytes=64)
             nc.vector.quantize_mx(
                 out=codes[:].bitcast(E5M2_X4),
                 scales=scales[:],
-                in_=grouped[:].rearrange("p t s w -> p (t s w)"),
+                in_=grouped[:].rearrange("p n s w -> p (n s w)"),
             )
-            return codes, scales
+            for i, g in enumerate(passes):
+                for t, ts in enumerate(tokens):
+                    place = i * len(tokens) + t
+                    quantised_of[b, g, ts] = (codes, scales, slice(place * P, (place + 1) * P))
+            for ts in tokens:
+                if all((b, g, ts) in quantised_of for g in range(PASSES)):
+                    operands = [quantised_of[b, g, ts] for g in range(PASSES)]
+                    waiting.extend((b, ts, n, operands) for n in range(N_TILES))
 
-        def multiply_and_store(b, ts, operands):
-            out_sb = work.tile([P, C], F32)
-            tokens = slice(ts % TU * P, (ts % TU + 1) * P)
-            for n in range(N_TILES):
-                cols = slice(n * N_TILE, (n + 1) * N_TILE)
-                acc = sums.tile([P, N_TILE], F32)
-                for g in range(PASSES):
-                    codes, scales = operands[g]
-                    nc.tensor.matmul_mx(
-                        out=acc[:],
-                        lhsT=codes[:, tokens].bitcast(E5M2_X4),
-                        lhsT_scale=scales[:, tokens],
-                        rhs=w_codes[:, g, cols].bitcast(E4M3_X4),
-                        rhs_scale=w_scales[:, g, cols],
-                        start=(g == 0),
-                        stop=(g == PASSES - 1),
-                    )
-                nc.scalar.copy(out=out_sb[:, cols], in_=acc[:])
-            nc.sync.dma_start(out=out[b].rearrange("(p t) c -> p t c", t=TS)[:, ts, :], in_=out_sb[:])
-
-        grouped_of = {}
-        quantised_of = {}
-        waiting = []
-        for step in range(len(UNITS) + LAG):
+        groups = {}
+        for step in range(STEPS):
             if step < len(UNITS):
-                grouped_of[step] = turn_add_round(*rope_products(step, mask(step)))
-            if WEIGHTS_FROM <= step < WEIGHTS_READY:
-                regroup_weights(step - WEIGHTS_FROM)
+                if step + MASK_LEAD in SCALAR_MASKS:
+                    scalar_mask(UNITS[step + MASK_LEAD])
+                unit = UNITS[step]
+                groups[step] = turn_add_round(unit, *rope_products(unit, mask(unit)))
+            for quarter, at in enumerate(REGROUP_STEP):
+                if step == at:
+                    regroup_weights(quarter)
             if step >= LAG:
-                b, g, tp = UNITS[step - LAG]
-                quantised_of[b, g, tp] = quantise_dy(grouped_of[step - LAG])
-                if all((b, other, tp) in quantised_of for other in range(PASSES)):
-                    for ts in range(tp * TU, (tp + 1) * TU):
-                        waiting.append((b, ts, [quantised_of[b, other, tp] for other in range(PASSES)]))
-            if step == WEIGHTS_READY:
-                for g in range(PASSES):
+                quantise_unit(UNITS[step - LAG], groups[step - LAG])
+            for g in range(PASSES):
+                if step == QUANTISE_STEP[g]:
                     quantise_weights(g)
-            if step >= WEIGHTS_READY:
-                for job in waiting[:CATCH_UP]:
-                    multiply_and_store(*job)
-                waiting = waiting[CATCH_UP:]
-        for job in waiting:
-            multiply_and_store(*job)
+            if step >= QUANTISE_STEP[-1]:
+                for b, ts, n, operands in waiting:
+                    spare = step >= len(UNITS) - 1 and n == 0
+                    multiply_bank(b, ts, n, operands, nc.vector.tensor_copy if spare else nc.scalar.copy)
+                waiting.clear()
+        assert not waiting

@@ -21,19 +21,19 @@ N_TILE = 512
 N_TILES = C // N_TILE
 
 UNITS = (
-    [(0, (g,), (0, 1)) for g in range(PASSES)]
+    [(0, (0,), (0,)), (0, (0,), (1,)), (0, (1,), (0, 1))]
     + [(b, (0, 1), (ts,)) for b in range(B) for ts in range(TS) if (b, ts) not in ((0, 0), (0, 1), (3, 3))]
     + [(3, (g,), (3,)) for g in range(PASSES)]
 )
 LOADS = (
-    [(0, (0,), (0, 1)), (0, (1,), (0, 1)), (0, (0, 1), (2, 3)), 0, 1]
+    [(0, (0,), (0,)), (0, (0,), (1,)), (0, (1,), (0, 1)), (0, (0, 1), (2,)), 0, (0, (0, 1), (3,)), 1]
     + [(1, (0, 1), (0, 1)), (1, (0, 1), (2, 3))]
     + [(b, (0, 1), (0, 1, 2, 3)) for b in (2, 3)]
 )
-LAG = 2
+LAG = 3
 STEPS = len(UNITS) + LAG
-SCALAR_MASKS = (1, 2, 6, 9, 12)
-MASK_LEAD = 1
+SCALAR_MASKS = (2, 3)
+MASK_LEAD = 2
 STEEP = 2.0**100
 STEP_BIAS = 64.0
 REGROUP_STEP = (1, 1, 2, 2)
@@ -85,7 +85,7 @@ def tile_lineartransformerblock_pa_v_kernel(tc, x, cos, sin, Wq, bq, r, grad_out
     with (
         tc.tile_pool(name="const", bufs=1) as const,
         tc.tile_pool(name="loads", bufs=1) as loads,
-        tc.tile_pool(name="work", bufs=4) as work,
+        tc.tile_pool(name="work", bufs=5) as work,
         tc.tile_pool(name="products", bufs=4) as products,
         tc.tile_pool(name="quantised", bufs=10) as quantised,
         tc.psum_pool(name="tables", bufs=1) as tables,
@@ -140,14 +140,14 @@ def tile_lineartransformerblock_pa_v_kernel(tc, x, cos, sin, Wq, bq, r, grad_out
             nc.vector.tensor_tensor(
                 out=own[:],
                 in0=dr[:],
-                in1=tab_own[:, cols].unsqueeze(1).to_broadcast([P, nh, nt * D]),
+                in1=(cos_sb[:] if unit == UNITS[0] else tab_own)[:, cols].unsqueeze(1).to_broadcast([P, nh, nt * D]),
                 op=ALU.mult,
             )
             swapped = dr[:].rearrange("p h (n e) -> p h n e", e=2)[:, :, :, ::-1]
-            split = nh - nh * 1 // 2
+            split = 3 if nh == H else 2
             for engine, table, hs in (
                 (nc.gpsimd, tab_pair_sb[:], slice(split, nh)),
-                (nc.vector, tab_pair, slice(0, split)),
+                (nc.vector, tab_pair_sb[:] if unit == UNITS[0] else tab_pair, slice(0, split)),
             ):
                 engine.tensor_tensor(
                     out=pair[:, hs].rearrange("p h (n e) -> p h n e", e=2),
@@ -182,10 +182,9 @@ def tile_lineartransformerblock_pa_v_kernel(tc, x, cos, sin, Wq, bq, r, grad_out
         def regroup_weights(quarter):
             g, half = divmod(quarter, 2)
             cols = slice(half * (C // 2), (half + 1) * (C // 2))
-            nc.scalar.copy(
-                out=w_grouped[:, g, cols, :].rearrange("p (c i) t -> p c t i", i=4),
-                in_=w_raw[:, g, :, cols].rearrange("p t (c i) -> p c t i", i=4),
-            )
+            grouped = w_grouped[:, g, cols, :].rearrange("p (c i) t -> p c t i", i=4)
+            raw = w_raw[:, g, :, cols].rearrange("p t (c i) -> p c t i", i=4)
+            nc.scalar.copy(out=grouped, in_=raw)
 
         def quantise_weights(g):
             nc.vector.quantize_mx(
@@ -211,10 +210,11 @@ def tile_lineartransformerblock_pa_v_kernel(tc, x, cos, sin, Wq, bq, r, grad_out
                     stop=(g == PASSES - 1),
                 )
             copy(out=out_tiles[b, ts][:, cols], in_=acc[:])
-            if n == N_TILES - 1:
-                nc.sync.dma_start(
-                    out=out[b].rearrange("(p t) c -> p t c", t=TS)[:, ts, :], in_=out_tiles[b, ts][:]
-                )
+            out_view = out[b].rearrange("(p t) c -> p t c", t=TS)[:, ts, :]
+            if b == B - 1 and ts >= TS - 2:
+                nc.sync.dma_start(out=out_view[:, cols], in_=out_tiles[b, ts][:, cols])
+            elif n == N_TILES - 1:
+                nc.sync.dma_start(out=out_view, in_=out_tiles[b, ts][:])
 
         out_tiles = {}
         quantised_of = {}
@@ -256,7 +256,7 @@ def tile_lineartransformerblock_pa_v_kernel(tc, x, cos, sin, Wq, bq, r, grad_out
                     quantise_weights(g)
             if step >= QUANTISE_STEP[-1]:
                 for b, ts, n, operands in waiting:
-                    spare = step >= len(UNITS) - 1 and n == 0
+                    spare = step >= STEPS - 1 and n == 0
                     multiply_bank(b, ts, n, operands, nc.vector.tensor_copy if spare else nc.scalar.copy)
                 waiting.clear()
         assert not waiting

@@ -46,8 +46,6 @@ BYTES = B * H * S * D * (4 + 2) + E * C * 2 + 2 * S * D * 2 + B * S * C * 4
 def load_inputs(nc, const, loads, cos, sin, Wq, r, grad_out):
     cos_sb = const.tile([P, TS * D], BF16)
     sin_sb = const.tile([P, TS * D], BF16)
-    nc.sync.dma_start(out=cos_sb[:], in_=cos.rearrange("(p t) d -> p (t d)", t=TS))
-    nc.sync.dma_start(out=sin_sb[:], in_=sin.rearrange("(p t) d -> p (t d)", t=TS))
     w_raw = const.tile([P, PASSES, PACK, C], BF16)
     w_view = Wq.rearrange("(g h p) c -> p g h c", g=PASSES, h=PACK)
     r_sb = [loads.tile([P, H, TS * D], F32, name=f"r_{b}") for b in range(B)]
@@ -63,6 +61,9 @@ def load_inputs(nc, const, loads, cos, sin, Wq, r, grad_out):
             for tile, src in ((r_sb[b], r), (g_sb[b], grad_out)):
                 view = src[b].rearrange("h (p t) d -> p h (t d)", t=TS)
                 nc.sync.dma_start(out=tile[:, heads, cols], in_=view[:, heads, cols])
+        if item == LOADS[0]:
+            nc.sync.dma_start(out=cos_sb[:], in_=cos.rearrange("(p t) d -> p (t d)", t=TS))
+            nc.sync.dma_start(out=sin_sb[:], in_=sin.rearrange("(p t) d -> p (t d)", t=TS))
     return cos_sb, sin_sb, w_raw, r_sb, g_sb
 
 

import concourse.mybir as mybir
from concourse.masks import make_identity

F32 = mybir.dt.float32
BF16 = mybir.dt.bfloat16
U32 = mybir.dt.uint32
U8 = mybir.dt.uint8
E4M3_X4 = mybir.dt.float8_e4m3fn_x4
E5M2_X4 = mybir.dt.float8_e5m2_x4
ALU = mybir.AluOpType
ACT = mybir.ActivationFunctionType

B, H, S, D, C = 4, 8, 512, 128, 1024
E = H * D
P = 128
TS = S // P
PACK = 4
PASSES = E // (P * PACK)
HP = H // PASSES
N_TILE = 512
N_TILES = C // N_TILE

UNITS = (
    [(0, (0,), (0,)), (0, (0,), (1,)), (0, (1,), (0, 1))]
    + [(b, (0, 1), (ts,)) for b in range(B) for ts in range(TS) if (b, ts) not in ((0, 0), (0, 1), (3, 3))]
    + [(3, (g,), (3,)) for g in range(PASSES)]
)
LOADS = (
    [(0, (0,), (0,)), (0, (0,), (1,)), (0, (1,), (0, 1)), (0, (0, 1), (2,)), 0, (0, (0, 1), (3,)), 1]
    + [(1, (0, 1), (0, 1)), (1, (0, 1), (2, 3))]
    + [(b, (0, 1), (0, 1, 2, 3)) for b in (2, 3)]
)
LAG = 3
STEPS = len(UNITS) + LAG
SCALAR_MASKS = (2, 3)
MASK_LEAD = 2
STEEP = 2.0**100
STEP_BIAS = 64.0
REGROUP_STEP = (1, 1, 2, 2)
QUANTISE_STEP = (4, 5)

FLOPS = 2 * B * S * E * C
BYTES = B * H * S * D * (4 + 2) + E * C * 2 + 2 * S * D * 2 + B * S * C * 4


def load_inputs(nc, const, loads, cos, sin, Wq, r, grad_out):
    cos_sb = const.tile([P, TS * D], BF16)
    sin_sb = const.tile([P, TS * D], BF16)
    w_raw = const.tile([P, PASSES, PACK, C], BF16)
    w_view = Wq.rearrange("(g h p) c -> p g h c", g=PASSES, h=PACK)
    r_sb = [loads.tile([P, H, TS * D], F32, name=f"r_{b}") for b in range(B)]
    g_sb = [loads.tile([P, H, TS * D], BF16, name=f"g_{b}") for b in range(B)]
    for item in LOADS:
        if isinstance(item, int):
            nc.sync.dma_start(out=w_raw[:, item], in_=w_view[:, item])
            continue
        b, passes, tokens = item
        cols = slice(tokens[0] * D, (tokens[-1] + 1) * D)
        for g in passes:
            heads = slice(g * HP, (g + 1) * HP)
            for tile, src in ((r_sb[b], r), (g_sb[b], grad_out)):
                view = src[b].rearrange("h (p t) d -> p h (t d)", t=TS)
                nc.sync.dma_start(out=tile[:, heads, cols], in_=view[:, heads, cols])
        if item == LOADS[0]:
            nc.sync.dma_start(out=cos_sb[:], in_=cos.rearrange("(p t) d -> p (t d)", t=TS))
            nc.sync.dma_start(out=sin_sb[:], in_=sin.rearrange("(p t) d -> p (t d)", t=TS))
    return cos_sb, sin_sb, w_raw, r_sb, g_sb


def make_rope_tables(nc, const, tables, cos_sb, sin_sb):
    pair_sb = const.tile([P, TS * D], BF16)
    pair_view = pair_sb[:].rearrange("p (n e) -> p n e", e=2)
    sin_view = sin_sb[:].rearrange("p (n e) -> p n e", e=2)
    identity_bf16 = const.tile([P, P], BF16)
    make_identity(nc, identity_bf16[:])
    nc.scalar.copy(out=pair_view[:, :, 0], in_=sin_view[:, :, 1])
    nc.scalar.activation(out=pair_view[:, :, 1], in_=sin_view[:, :, 0], func=ACT.Copy, scale=-1.0)
    both = tables.tile([P, 2, TS * D], BF16)
    for which, table_sb in enumerate((cos_sb, pair_sb)):
        nc.tensor.matmul(out=both[:, which], lhsT=identity_bf16[:], rhs=table_sb[:], start=True, stop=True)
    return both[:, 0], both[:, 1], pair_sb


def tile_lineartransformerblock_pa_v_kernel(tc, x, cos, sin, Wq, bq, r, grad_out, out):
    nc = tc.nc
    with (
        tc.tile_pool(name="const", bufs=1) as const,
        tc.tile_pool(name="loads", bufs=1) as loads,
        tc.tile_pool(name="work", bufs=5) as work,
        tc.tile_pool(name="products", bufs=4) as products,
        tc.tile_pool(name="quantised", bufs=10) as quantised,
        tc.psum_pool(name="tables", bufs=1) as tables,
        tc.psum_pool(name="turned", bufs=4) as turned,
        tc.psum_pool(name="sums", bufs=3) as sums,
    ):
        cos_sb, sin_sb, w_raw, r_sb, g_sb = load_inputs(nc, const, loads, cos, sin, Wq, r, grad_out)
        tab_own, tab_pair, tab_pair_sb = make_rope_tables(nc, const, tables, cos_sb, sin_sb)
        identity = const.tile([P, P], F32)
        make_identity(nc, identity[:])
        w_grouped = const.tile([P, PASSES, C, PACK], BF16, align_bytes=64)
        w_codes = const.tile([P, PASSES, C], U32, align_bytes=64)
        w_scales = const.tile([P, PASSES, C], U8, align_bytes=64)

        def parts(unit):
            b, passes, tokens = unit
            heads = slice(passes[0] * HP, (passes[-1] + 1) * HP)
            cols = slice(tokens[0] * D, (tokens[-1] + 1) * D)
            return b, heads, cols, len(passes) * HP, len(tokens)

        positives = {}

        def scalar_mask(unit):
            b, heads, cols, nh, nt = parts(unit)
            positives[unit] = work.tile([P, nh, nt * D], BF16, name="positive")
            nc.scalar.activation(
                out=positives[unit][:], in_=r_sb[b][:, heads, cols], func=ACT.Sigmoid, scale=STEEP, bias=-STEP_BIAS
            )

        def mask(unit):
            b, heads, cols, nh, nt = parts(unit)
            dr = work.tile([P, nh, nt * D], BF16)
            if unit in positives:
                nc.vector.tensor_tensor(
                    out=dr[:], in0=positives[unit][:], in1=g_sb[b][:, heads, cols], op=ALU.mult
                )
                return dr
            nc.vector.scalar_tensor_tensor(
                out=dr[:],
                in0=r_sb[b][:, heads, cols],
                scalar=0.0,
                in1=g_sb[b][:, heads, cols],
                op0=ALU.is_gt,
                op1=ALU.mult,
            )
            return dr

        def rope_products(unit, dr):
            b, heads, cols, nh, nt = parts(unit)
            own = products.tile([P, nh, nt * D], F32)
            pair = products.tile([P, nh, nt * D], F32)
            nc.vector.tensor_tensor(
                out=own[:],
                in0=dr[:],
                in1=(cos_sb[:] if unit == UNITS[0] else tab_own)[:, cols].unsqueeze(1).to_broadcast([P, nh, nt * D]),
                op=ALU.mult,
            )
            swapped = dr[:].rearrange("p h (n e) -> p h n e", e=2)[:, :, :, ::-1]
            split = 3 if nh == H else 2
            for engine, table, hs in (
                (nc.gpsimd, tab_pair_sb[:], slice(split, nh)),
                (nc.vector, tab_pair_sb[:] if unit == UNITS[0] else tab_pair, slice(0, split)),
            ):
                engine.tensor_tensor(
                    out=pair[:, hs].rearrange("p h (n e) -> p h n e", e=2),
                    in0=swapped[:, hs],
                    in1=table[:, cols]
                    .rearrange("p (n e) -> p n e", e=2)
                    .unsqueeze(1)
                    .to_broadcast([P, hs.stop - hs.start, nt * D // 2, 2]),
                    op=ALU.mult,
                )
            return own, pair

        def turn_add_round(unit, own, pair):
            b, passes, tokens = unit
            grouped = work.tile([P, len(passes) * len(tokens), P, PACK], BF16, align_bytes=64)
            for i, g in enumerate(passes):
                for t in range(len(tokens)):
                    dy_t = turned.tile([P, PACK, P], F32)
                    for h in range(HP):
                        for product, start in ((own, True), (pair, False)):
                            nc.tensor.matmul(
                                out=dy_t[:, h, :],
                                lhsT=product[:, i * HP + h, t * D : (t + 1) * D],
                                rhs=identity[:],
                                is_transpose=True,
                                start=start,
                                stop=not start,
                            )
                    nc.scalar.copy(out=grouped[:, i * len(tokens) + t], in_=dy_t[:].rearrange("p w s -> p s w"))
            return grouped

        def regroup_weights(quarter):
            g, half = divmod(quarter, 2)
            cols = slice(half * (C // 2), (half + 1) * (C // 2))
            grouped = w_grouped[:, g, cols, :].rearrange("p (c i) t -> p c t i", i=4)
            raw = w_raw[:, g, :, cols].rearrange("p t (c i) -> p c t i", i=4)
            nc.scalar.copy(out=grouped, in_=raw)

        def quantise_weights(g):
            nc.vector.quantize_mx(
                out=w_codes[:, g, :].bitcast(E4M3_X4),
                scales=w_scales[:, g, :],
                in_=w_grouped[:, g].rearrange("p c t -> p (c t)"),
            )

        def multiply_bank(b, ts, n, operands, copy):
            cols = slice(n * N_TILE, (n + 1) * N_TILE)
            if n == 0:
                out_tiles[b, ts] = work.tile([P, C], F32, name="out_sb")
            acc = sums.tile([P, N_TILE], F32)
            for g in range(PASSES):
                codes, scales, words = operands[g]
                nc.tensor.matmul_mx(
                    out=acc[:],
                    lhsT=codes[:, words].bitcast(E5M2_X4),
                    lhsT_scale=scales[:, words],
                    rhs=w_codes[:, g, cols].bitcast(E4M3_X4),
                    rhs_scale=w_scales[:, g, cols],
                    start=(g == 0),
                    stop=(g == PASSES - 1),
                )
            copy(out=out_tiles[b, ts][:, cols], in_=acc[:])
            out_view = out[b].rearrange("(p t) c -> p t c", t=TS)[:, ts, :]
            if b == B - 1 and ts >= TS - 2:
                nc.sync.dma_start(out=out_view[:, cols], in_=out_tiles[b, ts][:, cols])
            elif n == N_TILES - 1:
                nc.sync.dma_start(out=out_view, in_=out_tiles[b, ts][:])

        out_tiles = {}
        quantised_of = {}
        waiting = []

        def quantise_unit(unit, grouped):
            b, passes, tokens = unit
            n = grouped.shape[1]
            codes = quantised.tile([P, n * P], U32, align_bytes=64)
            scales = quantised.tile([P, n * P], U8, align_bytes=64)
            nc.vector.quantize_mx(
                out=codes[:].bitcast(E5M2_X4),
                scales=scales[:],
                in_=grouped[:].rearrange("p n s w -> p (n s w)"),
            )
            for i, g in enumerate(passes):
                for t, ts in enumerate(tokens):
                    place = i * len(tokens) + t
                    quantised_of[b, g, ts] = (codes, scales, slice(place * P, (place + 1) * P))
            for ts in tokens:
                if all((b, g, ts) in quantised_of for g in range(PASSES)):
                    operands = [quantised_of[b, g, ts] for g in range(PASSES)]
                    waiting.extend((b, ts, n, operands) for n in range(N_TILES))

        groups = {}
        for step in range(STEPS):
            if step < len(UNITS):
                if step + MASK_LEAD in SCALAR_MASKS:
                    scalar_mask(UNITS[step + MASK_LEAD])
                unit = UNITS[step]
                groups[step] = turn_add_round(unit, *rope_products(unit, mask(unit)))
            for quarter, at in enumerate(REGROUP_STEP):
                if step == at:
                    regroup_weights(quarter)
            if step >= LAG:
                quantise_unit(UNITS[step - LAG], groups[step - LAG])
            for g in range(PASSES):
                if step == QUANTISE_STEP[g]:
                    quantise_weights(g)
            if step >= QUANTISE_STEP[-1]:
                for b, ts, n, operands in waiting:
                    spare = step >= STEPS - 1 and n == 0
                    multiply_bank(b, ts, n, operands, nc.vector.tensor_copy if spare else nc.scalar.copy)
                waiting.clear()
        assert not waiting
